import numpy as np
import ml_dtypes


def mxq(x, axis, fmt="e4m3"):
    dtype, down = {"e4m3": (ml_dtypes.float8_e4m3fn, 7), "e5m2": (ml_dtypes.float8_e5m2, 14)}[fmt]
    v = np.moveaxis(np.asarray(x, np.float32).astype(ml_dtypes.bfloat16).astype(np.float64), axis, -1)
    blocks = v.reshape(v.shape[:-1] + (-1, 32))
    amax = np.abs(blocks).max(-1, keepdims=True)
    byte = np.maximum(np.where(amax > 0, np.frexp(amax)[1] - 1 + 127, 0) - down, 1)
    scale = np.exp2(byte - 127.0)
    codes = (blocks / scale).astype(np.float32).astype(dtype).astype(np.float64)
    return np.moveaxis((codes * scale).reshape(v.shape), -1, axis)


WIDE = False


def mx_kscale(k):
    if not WIDE:
        return np.ones(k)
    levels = np.array([20, -20, 10, -10, 0])
    a = np.random.permutation(np.resize(levels, k // 512 * 4)).reshape(k // 512, 4)
    idx = np.arange(k)
    return np.exp2(a[idx // 512, idx % 128 // 32])


BF16 = ml_dtypes.bfloat16


def bf(x):
    return np.asarray(x, np.float32).astype(BF16)


def f64(x):
    return np.asarray(x).astype(np.float64)


B, C, O, ROWS, COLS, KH, KW = 512, 64, 512, 3, 3, 4, 4
H, W, K = ROWS + KH - 1, COLS + KW - 1, C * KH * KW


def patch_matrices(x, rows, cols, kh, kw):
    b, c = x.shape[:2]
    patches = np.stack(
        [np.stack([x[:, :, u:u + rows, v:v + cols] for v in range(kw)], axis=2)
         for u in range(kh)], axis=2)
    return patches.transpose(4, 5, 0, 1, 2, 3).reshape(rows * cols, b, c * kh * kw)


def setup_inputs():
    s = mx_kscale(B)[:, None, None, None]
    x = np.random.standard_normal((B, C, H, W)) * s
    weight = np.random.standard_normal((ROWS, COLS, O, C, KH, KW)) / np.sqrt(K)
    g = np.random.standard_normal((B, O, ROWS, COLS)) * np.exp2(np.random.randint(-12, 1, (B, 1, ROWS, COLS))) / s
    return {"x": bf(x), "weight": bf(weight), "grad_out": bf(g)}


def reference(x, weight, grad_out):
    rows, cols, o, c, kh, kw = weight.shape
    b = x.shape[0]
    xq = mxq(f64(x), 0, "e4m3")
    gq = mxq(f64(grad_out), 0, "e5m2")
    p = patch_matrices(xq, rows, cols, kh, kw)
    g = gq.transpose(2, 3, 0, 1).reshape(rows * cols, b, o)
    gw = g.transpose(0, 2, 1) @ p
    return gw.reshape(rows, cols, o, c, kh, kw)

@@ -1,0 +1,199 @@
+from contextlib import ExitStack
+
+import concourse.mybir as mybir
+
+F32 = mybir.dt.float32
+BF16 = mybir.dt.bfloat16
+U32 = mybir.dt.uint32
+U8 = mybir.dt.uint8
+E4M3X4 = mybir.dt.float8_e4m3fn_x4
+E5M2X4 = mybir.dt.float8_e5m2_x4
+
+P = 128
+PACK = 4
+B = 512
+C = 64
+O = 512
+ROWS = 3
+COLS = 3
+KH = 4
+KW = 4
+H = 6
+W = 6
+N_WIN = 512
+ROW_COLS = C * KW
+R = 2
+CHUNK = P * R
+N_CHUNKS = O // CHUNK
+UNITS = ROWS * COLS * N_CHUNKS
+BLOCK = ROWS
+N_BLOCKS = UNITS // BLOCK
+
+FLOPS = 2 * ROWS * COLS * O * C * KH * KW * B
+BYTES = 2 * B * C * H * W + 2 * B * O * ROWS * COLS + 4 * ROWS * COLS * O * C * KH * KW
+
+MANUAL = False
+V_SHARE = [0] * 12 + [1, 1, 1, 2, 2, 2]
+
+
+def tile_localconvolution_kernel(tc, x, weight, grad_out, out):
+    nc = tc.nc
+    with ExitStack() as ctx:
+        if MANUAL:
+            ctx.enter_context(tc.manual_schedule())
+        raw = ctx.enter_context(tc.tile_pool(name="raw", bufs=1))
+        keep = ctx.enter_context(tc.tile_pool(name="keep", bufs=1))
+        gstage = ctx.enter_context(tc.tile_pool(name="gstage", bufs=2))
+        res = ctx.enter_context(tc.tile_pool(name="res", bufs=8))
+        psum = ctx.enter_context(tc.psum_pool(name="psum", bufs=8))
+
+        xraw = raw.tile([P, PACK, C * H * W], BF16)
+        nc.sync.dma_start(out=xraw[:], in_=x.rearrange("(p t) c h w -> p t (c h w)", t=PACK))
+        graw = []
+        for k in range(N_CHUNKS):
+            g_t = raw.tile([P, PACK, CHUNK * ROWS * COLS], BF16, name="graw%d" % k)
+            nc.sync.dma_start(
+                out=g_t[:],
+                in_=grad_out[:, k * CHUNK : (k + 1) * CHUNK].rearrange(
+                    "(p t) o i j -> p t (o i j)", t=PACK
+                ),
+            )
+            graw.append(g_t)
+
+        xg = []
+        xcodes = []
+        xscales = []
+        for j in range(COLS):
+            xg.append(
+                (
+                    keep.tile([P, 4, C, KW, PACK], BF16, name="xga%d" % j, align_bytes=64),
+                    keep.tile([P, 2, C, KW, PACK], BF16, name="xgb%d" % j, align_bytes=64),
+                )
+            )
+            xcodes.append(keep.tile([P, H * ROW_COLS], U32, name="xcodes%d" % j, align_bytes=64))
+            xscales.append(keep.tile([P, H * ROW_COLS], U8, name="xscales%d" % j, align_bytes=64))
+        x_view = xraw[:].rearrange("p t (c h w) -> p h c t w", c=C, h=H, w=W)
+
+        def regroup_x(copy, j, h):
+            part = xg[j][h // 4]
+            copy(
+                out=part[:, h % 4].rearrange("p c v t -> p c t v"),
+                in_=x_view[:, h, :, :, j : j + KW],
+            )
+
+        def quantise_x(j, part):
+            lo = 0 if part == 0 else 4 * ROW_COLS
+            hi = 4 * ROW_COLS if part == 0 else H * ROW_COLS
+            nc.vector.quantize_mx(
+                out=xcodes[j][:, lo:hi].bitcast(E4M3X4),
+                scales=xscales[j][:, lo:hi],
+                in_=xg[j][part][:].rearrange("p r c v t -> p (r c v t)"),
+            )
+
+        slot_home = {}
+
+        def unit_place(u):
+            j = u // (BLOCK * N_CHUNKS)
+            k = (u // BLOCK) % N_CHUNKS
+            i = u % BLOCK
+            return i, j, k
+
+        def open_group(name, slots):
+            n = len(slots)
+            gg = gstage.tile([P, n, P, PACK], BF16, name="gg_" + name, tag="gg%d" % n, align_bytes=64)
+            gc = keep.tile([P, n * P], U32, name="gc_" + name, align_bytes=64)
+            gs = keep.tile([P, n * P], U8, name="gs_" + name, align_bytes=64)
+            for m in range(n):
+                slot_home[slots[m]] = (gg, gc, gs, m)
+            return gg, gc, gs
+
+        def regroup_g(s, n):
+            i, j, k = unit_place(s // R)
+            gg, gc, gs, m = slot_home[s]
+            src = graw[k][:].rearrange("p t (q r s) -> p s r q t", q=P, r=R, s=ROWS * COLS)
+            nc.vector.tensor_copy(
+                out=gg[:, m : m + n],
+                in_=src[:, i * COLS + j, s % R : s % R + n],
+            )
+
+        def quantise_g(group):
+            gg, gc, gs = group
+            nc.vector.quantize_mx(
+                out=gc[:].bitcast(E5M2X4),
+                scales=gs[:],
+                in_=gg[:].rearrange("p n q t -> p (n q t)"),
+            )
+
+        def unit(u):
+            i, j, k = unit_place(u)
+            share = V_SHARE[u]
+            res_t = res.tile([P, R, C * KH * KW], F32, tag="res")
+            dst = out[i, j, k * CHUNK : (k + 1) * CHUNK].rearrange("(q r) c u v -> q r (c u v)", r=R)
+            for r in range(R):
+                gg, gc, gs, m = slot_home[R * u + r]
+                for w in range(2):
+                    acc = psum.tile([P, N_WIN], F32, tag="acc")
+                    lo = (i + 2 * w) * ROW_COLS
+                    nc.tensor.matmul_mx(
+                        out=acc[:],
+                        lhsT=gc[:, m * P : (m + 1) * P].bitcast(E5M2X4),
+                        lhsT_scale=gs[:, m * P : (m + 1) * P],
+                        rhs=xcodes[j][:, lo : lo + N_WIN].bitcast(E4M3X4),
+                        rhs_scale=xscales[j][:, lo : lo + N_WIN],
+                        start=True,
+                        stop=True,
+                    )
+                    on_vector = (share == 2 and w == 1) or (share == 1 and r == 1 and w == 1)
+                    copy = nc.vector.tensor_copy if on_vector else nc.scalar.copy
+                    copy(
+                        out=res_t[:, r].rearrange("p (c u v) -> p c u v", c=C, u=KH, v=KW)[
+                            :, :, 2 * w : 2 * w + 2, :
+                        ],
+                        in_=acc[:].rearrange("p (u c v) -> p c u v", u=2, c=C, v=KW),
+                    )
+                if u == 0:
+                    nc.sync.dma_start(out=dst[:, r], in_=res_t[:, r])
+            if u > 0:
+                nc.sync.dma_start(out=dst, in_=res_t[:])
+
+        for h in range(H):
+            regroup_x(nc.vector.tensor_copy, 0, h)
+        for h in range(H):
+            regroup_x(nc.scalar.copy, 1, h)
+        quantise_x(0, 0)
+        quantise_x(0, 1)
+        first0 = open_group("b0s0", [0])
+        first1 = open_group("b0s1", [1])
+        rest0 = open_group("b0b", [2, 3, 4, 5])
+        regroup_g(0, 1)
+        quantise_g(first0)
+        regroup_g(1, 1)
+        quantise_g(first1)
+        regroup_g(2, 2)
+        regroup_g(4, 2)
+        quantise_g(rest0)
+        groups = {}
+        for u in range(UNITS):
+            nb = u // BLOCK + 1
+            pos = u % BLOCK
+            if nb < N_BLOCKS:
+                s0 = R * BLOCK * nb
+                if pos == 0:
+                    groups[(nb, 0)] = open_group("b%da" % nb, [s0, s0 + 1])
+                    groups[(nb, 1)] = open_group("b%db" % nb, [s0 + 2, s0 + 3, s0 + 4, s0 + 5])
+                regroup_g(s0 + R * pos, 2)
+            if u == 1:
+                quantise_x(1, 0)
+            if u == 2:
+                quantise_x(1, 1)
+            if 3 <= u <= 8:
+                regroup_x(nc.vector.tensor_copy, 2, u - 3)
+            if u == 9:
+                quantise_x(2, 0)
+            if u == 10:
+                quantise_x(2, 1)
+            if nb < N_BLOCKS and pos == 1:
+                quantise_g(groups[(nb, 0)])
+            unit(u)
+            if nb < N_BLOCKS and pos == 2:
+                quantise_g(groups[(nb, 1)])

@@ -32,7 +32,7 @@ N_BLOCKS = UNITS // BLOCK
 FLOPS = 2 * ROWS * COLS * O * C * KH * KW * B
 BYTES = 2 * B * C * H * W + 2 * B * O * ROWS * COLS + 4 * ROWS * COLS * O * C * KH * KW
 
-MANUAL = False
+MANUAL = True
 V_SHARE = [0] * 12 + [1, 1, 1, 2, 2, 2]
 
 

@@ -22,41 +22,46 @@ H = 6
 W = 6
 N_WIN = 512
 ROW_COLS = C * KW
-R = 2
-CHUNK = P * R
-N_CHUNKS = O // CHUNK
-UNITS = ROWS * COLS * N_CHUNKS
-BLOCK = ROWS
-N_BLOCKS = UNITS // BLOCK
+IJ = ROWS * COLS
+C_HALF = C // 2
 
 FLOPS = 2 * ROWS * COLS * O * C * KH * KW * B
 BYTES = 2 * B * C * H * W + 2 * B * O * ROWS * COLS + 4 * ROWS * COLS * O * C * KH * KW
 
-MANUAL = True
-V_SHARE = [0] * 12 + [1, 1, 1, 2, 2, 2]
+LOOKAHEAD = 2
+V_SHARE = [0, 0, 0, 0, 0, 0, 0, 1, 0, 0, 0, 0, 0, 0, 0, 0, 1, 1, 1, 1, 2]
+X1_QUANT = (2, 3)
+X2_ROWS = (9, 10, 11, 12, 13, 13)
+X2_QUANT = (13, 14)
+GROUP_SIZES = [1, 1, 2, 2, 2, 4] + [2, 4] * 4
 
 
 def tile_localconvolution_kernel(tc, x, weight, grad_out, out):
     nc = tc.nc
     with ExitStack() as ctx:
-        if MANUAL:
-            ctx.enter_context(tc.manual_schedule())
+        ctx.enter_context(tc.manual_schedule())
         raw = ctx.enter_context(tc.tile_pool(name="raw", bufs=1))
         keep = ctx.enter_context(tc.tile_pool(name="keep", bufs=1))
         gstage = ctx.enter_context(tc.tile_pool(name="gstage", bufs=2))
         res = ctx.enter_context(tc.tile_pool(name="res", bufs=8))
         psum = ctx.enter_context(tc.psum_pool(name="psum", bufs=8))
 
-        xraw = raw.tile([P, PACK, C * H * W], BF16)
-        nc.sync.dma_start(out=xraw[:], in_=x.rearrange("(p t) c h w -> p t (c h w)", t=PACK))
+        x_view = []
+        for half in range(2):
+            x_t = raw.tile([P, PACK, C_HALF * H * W], BF16, name="xraw%d" % half)
+            nc.sync.dma_start(
+                out=x_t[:],
+                in_=x[:, half * C_HALF : (half + 1) * C_HALF].rearrange(
+                    "(p t) c h w -> p t (c h w)", t=PACK
+                ),
+            )
+            x_view.append(x_t[:].rearrange("p t (c h w) -> p h c t w", c=C_HALF, h=H, w=W))
         graw = []
-        for k in range(N_CHUNKS):
-            g_t = raw.tile([P, PACK, CHUNK * ROWS * COLS], BF16, name="graw%d" % k)
+        for lo, hi in ((0, P), (P, 2 * P), (2 * P, O)):
+            g_t = raw.tile([P, PACK, (hi - lo) * IJ], BF16, name="graw%d" % lo)
             nc.sync.dma_start(
                 out=g_t[:],
-                in_=grad_out[:, k * CHUNK : (k + 1) * CHUNK].rearrange(
-                    "(p t) o i j -> p t (o i j)", t=PACK
-                ),
+                in_=grad_out[:, lo:hi].rearrange("(p t) o i j -> p t (o i j)", t=PACK),
             )
             graw.append(g_t)
 
@@ -72,13 +77,14 @@ def tile_localconvolution_kernel(tc, x, weight, grad_out, out):
             )
             xcodes.append(keep.tile([P, H * ROW_COLS], U32, name="xcodes%d" % j, align_bytes=64))
             xscales.append(keep.tile([P, H * ROW_COLS], U8, name="xscales%d" % j, align_bytes=64))
-        x_view = xraw[:].rearrange("p t (c h w) -> p h c t w", c=C, h=H, w=W)
 
-        def regroup_x(copy, j, h):
+        def regroup_x(copy, j, h, half):
             part = xg[j][h // 4]
             copy(
-                out=part[:, h % 4].rearrange("p c v t -> p c t v"),
-                in_=x_view[:, h, :, :, j : j + KW],
+                out=part[:, h % 4, half * C_HALF : (half + 1) * C_HALF].rearrange(
+                    "p c v t -> p c t v"
+                ),
+                in_=x_view[half][:, h, :, :, j : j + KW],
             )
 
         def quantise_x(j, part):
@@ -90,47 +96,69 @@ def tile_localconvolution_kernel(tc, x, weight, grad_out, out):
                 in_=xg[j][part][:].rearrange("p r c v t -> p (r c v t)"),
             )
 
-        slot_home = {}
+        units = []
+        for o0 in (0, P):
+            for i in range(ROWS):
+                units.append((i, 0, o0, 1))
+        for i in range(ROWS):
+            units.append((i, 0, 2 * P, 2))
+        for j in range(1, COLS):
+            for o0 in (0, 2 * P):
+                for i in range(ROWS):
+                    units.append((i, j, o0, 2))
+        first_slot = []
+        n_slots = 0
+        for u in units:
+            first_slot.append(n_slots)
+            n_slots += u[3]
+        assert n_slots == sum(GROUP_SIZES)
 
-        def unit_place(u):
-            j = u // (BLOCK * N_CHUNKS)
-            k = (u // BLOCK) % N_CHUNKS
-            i = u % BLOCK
-            return i, j, k
-
-        def open_group(name, slots):
-            n = len(slots)
-            gg = gstage.tile([P, n, P, PACK], BF16, name="gg_" + name, tag="gg%d" % n, align_bytes=64)
-            gc = keep.tile([P, n * P], U32, name="gc_" + name, align_bytes=64)
-            gs = keep.tile([P, n * P], U8, name="gs_" + name, align_bytes=64)
+        slot_home = []
+        groups = []
+        for n in GROUP_SIZES:
             for m in range(n):
-                slot_home[slots[m]] = (gg, gc, gs, m)
-            return gg, gc, gs
+                slot_home.append((len(groups), m))
+            groups.append([n, None, None, None, 0])
 
-        def regroup_g(s, n):
-            i, j, k = unit_place(s // R)
-            gg, gc, gs, m = slot_home[s]
-            src = graw[k][:].rearrange("p t (q r s) -> p s r q t", q=P, r=R, s=ROWS * COLS)
-            nc.vector.tensor_copy(
-                out=gg[:, m : m + n],
-                in_=src[:, i * COLS + j, s % R : s % R + n],
-            )
+        def regroup_g(t):
+            i, j, o0, r = units[t]
+            ij = i * COLS + j
+            k, m = slot_home[first_slot[t]]
+            grp = groups[k]
+            if grp[1] is None:
+                n = grp[0]
+                grp[1] = gstage.tile([P, n, P, PACK], BF16, name="gg%d" % k, tag="gg%d" % n, align_bytes=64)
+                grp[2] = keep.tile([P, n * P], U32, name="gc%d" % k, align_bytes=64)
+                grp[3] = keep.tile([P, n * P], U8, name="gs%d" % k, align_bytes=64)
+            gg = grp[1]
+            if r == 1:
+                src = graw[o0 // P][:].rearrange("p t (q s) -> p s q t", q=P, s=IJ)
+                nc.vector.tensor_copy(out=gg[:, m], in_=src[:, ij])
+            elif o0 == 2 * P:
+                src = graw[2][:].rearrange("p t (q r s) -> p s r q t", q=P, r=2, s=IJ)
+                nc.vector.tensor_copy(out=gg[:, m : m + 2], in_=src[:, ij])
+            else:
+                for a in range(2):
+                    src = graw[a][:].rearrange("p t (q r s) -> p s r q t", q=P // 2, r=2, s=IJ)
+                    nc.vector.tensor_copy(
+                        out=gg[:, m : m + 2, a * (P // 2) : (a + 1) * (P // 2)], in_=src[:, ij]
+                    )
+            grp[4] += r
+            if grp[4] == grp[0]:
+                nc.vector.quantize_mx(
+                    out=grp[2][:].bitcast(E5M2X4),
+                    scales=grp[3][:],
+                    in_=gg[:].rearrange("p n q t -> p (n q t)"),
+                )
 
-        def quantise_g(group):
-            gg, gc, gs = group
-            nc.vector.quantize_mx(
-                out=gc[:].bitcast(E5M2X4),
-                scales=gs[:],
-                in_=gg[:].rearrange("p n q t -> p (n q t)"),
-            )
-
-        def unit(u):
-            i, j, k = unit_place(u)
-            share = V_SHARE[u]
-            res_t = res.tile([P, R, C * KH * KW], F32, tag="res")
-            dst = out[i, j, k * CHUNK : (k + 1) * CHUNK].rearrange("(q r) c u v -> q r (c u v)", r=R)
-            for r in range(R):
-                gg, gc, gs, m = slot_home[R * u + r]
+        def unit(t):
+            i, j, o0, r_n = units[t]
+            share = V_SHARE[t]
+            res_t = res.tile([P, r_n, C * KH * KW], F32, tag="res")
+            for r in range(r_n):
+                k, m = slot_home[first_slot[t] + r]
+                gc = groups[k][2]
+                gs = groups[k][3]
                 for w in range(2):
                     acc = psum.tile([P, N_WIN], F32, tag="acc")
                     lo = (i + 2 * w) * ROW_COLS
@@ -143,7 +171,7 @@ def tile_localconvolution_kernel(tc, x, weight, grad_out, out):
                         start=True,
                         stop=True,
                     )
-                    on_vector = (share == 2 and w == 1) or (share == 1 and r == 1 and w == 1)
+                    on_vector = 2 * r + w >= 2 * r_n - share
                     copy = nc.vector.tensor_copy if on_vector else nc.scalar.copy
                     copy(
                         out=res_t[:, r].rearrange("p (c u v) -> p c u v", c=C, u=KH, v=KW)[
@@ -151,49 +179,34 @@ def tile_localconvolution_kernel(tc, x, weight, grad_out, out):
                         ],
                         in_=acc[:].rearrange("p (u c v) -> p c u v", u=2, c=C, v=KW),
                     )
-                if u == 0:
-                    nc.sync.dma_start(out=dst[:, r], in_=res_t[:, r])
-            if u > 0:
-                nc.sync.dma_start(out=dst, in_=res_t[:])
+            nc.sync.dma_start(
+                out=out[i, j, o0 : o0 + r_n * P].rearrange("(q r) c u v -> q r (c u v)", r=r_n),
+                in_=res_t[:],
+            )
 
-        for h in range(H):
-            regroup_x(nc.vector.tensor_copy, 0, h)
-        for h in range(H):
-            regroup_x(nc.scalar.copy, 1, h)
+        for half in range(2):
+            for h in range(H):
+                regroup_x(nc.vector.tensor_copy, 0, h, half)
+        for half in range(2):
+            for h in range(H):
+                regroup_x(nc.scalar.copy, 1, h, half)
         quantise_x(0, 0)
         quantise_x(0, 1)
-        first0 = open_group("b0s0", [0])
-        first1 = open_group("b0s1", [1])
-        rest0 = open_group("b0b", [2, 3, 4, 5])
-        regroup_g(0, 1)
-        quantise_g(first0)
-        regroup_g(1, 1)
-        quantise_g(first1)
-        regroup_g(2, 2)
-        regroup_g(4, 2)
-        quantise_g(rest0)
-        groups = {}
-        for u in range(UNITS):
-            nb = u // BLOCK + 1
-            pos = u % BLOCK
-            if nb < N_BLOCKS:
-                s0 = R * BLOCK * nb
-                if pos == 0:
-                    groups[(nb, 0)] = open_group("b%da" % nb, [s0, s0 + 1])
-                    groups[(nb, 1)] = open_group("b%db" % nb, [s0 + 2, s0 + 3, s0 + 4, s0 + 5])
-                regroup_g(s0 + R * pos, 2)
-            if u == 1:
-                quantise_x(1, 0)
-            if u == 2:
-                quantise_x(1, 1)
-            if 3 <= u <= 8:
-                regroup_x(nc.vector.tensor_copy, 2, u - 3)
-            if u == 9:
-                quantise_x(2, 0)
-            if u == 10:
-                quantise_x(2, 1)
-            if nb < N_BLOCKS and pos == 1:
-                quantise_g(groups[(nb, 0)])
-            unit(u)
-            if nb < N_BLOCKS and pos == 2:
-                quantise_g(groups[(nb, 1)])
+        for t in range(LOOKAHEAD):
+            regroup_g(t)
+        x2_row = 0
+        for t in range(len(units)):
+            if t + LOOKAHEAD < len(units):
+                regroup_g(t + LOOKAHEAD)
+            for part in range(2):
+                if t == X1_QUANT[part]:
+                    quantise_x(1, part)
+            for step in X2_ROWS:
+                if step == t:
+                    regroup_x(nc.vector.tensor_copy, 2, x2_row, 0)
+                    regroup_x(nc.vector.tensor_copy, 2, x2_row, 1)
+                    x2_row += 1
+            for part in range(2):
+                if t == X2_QUANT[part]:
+                    quantise_x(2, part)
+            unit(t)

@@ -28,12 +28,11 @@ C_HALF = C // 2
 FLOPS = 2 * ROWS * COLS * O * C * KH * KW * B
 BYTES = 2 * B * C * H * W + 2 * B * O * ROWS * COLS + 4 * ROWS * COLS * O * C * KH * KW
 
-LOOKAHEAD = 2
 V_SHARE = [0, 0, 0, 0, 0, 0, 0, 1, 0, 0, 0, 0, 0, 0, 0, 0, 1, 1, 1, 1, 2]
-X1_QUANT = (2, 3)
+X1_QUANT = (1, 2)
 X2_ROWS = (9, 10, 11, 12, 13, 13)
 X2_QUANT = (13, 14)
-GROUP_SIZES = [1, 1, 2, 2, 2, 4] + [2, 4] * 4
+BLOCKS = ((0, 0, 1), (0, P, 1), (1, 0, 2), (0, 2 * P, 2), (1, 2 * P, 2), (2, 0, 2), (2, 2 * P, 2))
 
 
 def tile_localconvolution_kernel(tc, x, weight, grad_out, out):
@@ -96,69 +95,50 @@ def tile_localconvolution_kernel(tc, x, weight, grad_out, out):
                 in_=xg[j][part][:].rearrange("p r c v t -> p (r c v t)"),
             )
 
-        units = []
-        for o0 in (0, P):
-            for i in range(ROWS):
-                units.append((i, 0, o0, 1))
-        for i in range(ROWS):
-            units.append((i, 0, 2 * P, 2))
-        for j in range(1, COLS):
-            for o0 in (0, 2 * P):
-                for i in range(ROWS):
-                    units.append((i, j, o0, 2))
-        first_slot = []
-        n_slots = 0
-        for u in units:
-            first_slot.append(n_slots)
-            n_slots += u[3]
-        assert n_slots == sum(GROUP_SIZES)
+        homes = []
 
-        slot_home = []
-        groups = []
-        for n in GROUP_SIZES:
-            for m in range(n):
-                slot_home.append((len(groups), m))
-            groups.append([n, None, None, None, 0])
-
-        def regroup_g(t):
-            i, j, o0, r = units[t]
-            ij = i * COLS + j
-            k, m = slot_home[first_slot[t]]
-            grp = groups[k]
-            if grp[1] is None:
-                n = grp[0]
-                grp[1] = gstage.tile([P, n, P, PACK], BF16, name="gg%d" % k, tag="gg%d" % n, align_bytes=64)
-                grp[2] = keep.tile([P, n * P], U32, name="gc%d" % k, align_bytes=64)
-                grp[3] = keep.tile([P, n * P], U8, name="gs%d" % k, align_bytes=64)
-            gg = grp[1]
-            if r == 1:
-                src = graw[o0 // P][:].rearrange("p t (q s) -> p s q t", q=P, s=IJ)
-                nc.vector.tensor_copy(out=gg[:, m], in_=src[:, ij])
-            elif o0 == 2 * P:
-                src = graw[2][:].rearrange("p t (q r s) -> p s r q t", q=P, r=2, s=IJ)
-                nc.vector.tensor_copy(out=gg[:, m : m + 2], in_=src[:, ij])
+        def prep_ops(b):
+            j, o0, r_n = BLOCKS[b]
+            gg = gstage.tile([P, ROWS * r_n, P, PACK], BF16, name="gg%d" % b, tag="gg%d" % r_n, align_bytes=64)
+            gc = keep.tile([P, ROWS * r_n * P], U32, name="gc%d" % b, align_bytes=64)
+            gs = keep.tile([P, ROWS * r_n * P], U8, name="gs%d" % b, align_bytes=64)
+            homes.append((gc, gs))
+            dst = gg[:].rearrange("p (i r) q t -> p r q t i", i=ROWS, r=r_n)
+            pieces = []
+            if o0 == 2 * P:
+                sources = ((graw[2], 0, P),)
+            elif r_n == 1:
+                sources = ((graw[o0 // P], 0, P),)
             else:
-                for a in range(2):
-                    src = graw[a][:].rearrange("p t (q r s) -> p s r q t", q=P // 2, r=2, s=IJ)
-                    nc.vector.tensor_copy(
-                        out=gg[:, m : m + 2, a * (P // 2) : (a + 1) * (P // 2)], in_=src[:, ij]
-                    )
-            grp[4] += r
-            if grp[4] == grp[0]:
+                sources = ((graw[0], 0, P // 2), (graw[1], P // 2, P))
+            for g_t, q_lo, q_hi in sources:
+                src = g_t[:].rearrange(
+                    "p t (q r i j) -> p r j q t i", q=q_hi - q_lo, r=r_n, i=ROWS, j=COLS
+                )
+                for r in range(r_n):
+                    pieces.append((dst[:, r, q_lo:q_hi], src[:, r, j]))
+
+            def quantise(lo, hi):
                 nc.vector.quantize_mx(
-                    out=grp[2][:].bitcast(E5M2X4),
-                    scales=grp[3][:],
-                    in_=gg[:].rearrange("p n q t -> p (n q t)"),
+                    out=gc[:, lo * P : hi * P].bitcast(E5M2X4),
+                    scales=gs[:, lo * P : hi * P],
+                    in_=gg[:, lo:hi].rearrange("p n q t -> p (n q t)"),
                 )
 
+            return pieces, quantise
+
+        def regroup_g(pieces):
+            for dst_ap, src_ap in pieces:
+                nc.vector.tensor_copy(out=dst_ap, in_=src_ap)
+
         def unit(t):
-            i, j, o0, r_n = units[t]
+            j, o0, r_n = BLOCKS[t // ROWS]
+            i = t % ROWS
+            gc, gs = homes[t // ROWS]
             share = V_SHARE[t]
             res_t = res.tile([P, r_n, C * KH * KW], F32, tag="res")
             for r in range(r_n):
-                k, m = slot_home[first_slot[t] + r]
-                gc = groups[k][2]
-                gs = groups[k][3]
+                m = i * r_n + r
                 for w in range(2):
                     acc = psum.tile([P, N_WIN], F32, tag="acc")
                     lo = (i + 2 * w) * ROW_COLS
@@ -192,12 +172,23 @@ def tile_localconvolution_kernel(tc, x, weight, grad_out, out):
                 regroup_x(nc.scalar.copy, 1, h, half)
         quantise_x(0, 0)
         quantise_x(0, 1)
-        for t in range(LOOKAHEAD):
-            regroup_g(t)
+        pieces, quantise = prep_ops(0)
+        regroup_g(pieces)
+        quantise(0, BLOCKS[0][2])
+        quantise(BLOCKS[0][2], ROWS * BLOCKS[0][2])
         x2_row = 0
-        for t in range(len(units)):
-            if t + LOOKAHEAD < len(units):
-                regroup_g(t + LOOKAHEAD)
+        for t in range(ROWS * len(BLOCKS)):
+            nxt = t // ROWS + 1
+            pos = t % ROWS
+            if nxt < len(BLOCKS):
+                if pos == 0:
+                    pieces, quantise = prep_ops(nxt)
+                    regroup_g(pieces[: (len(pieces) + 1) // 2])
+                elif pos == 1:
+                    regroup_g(pieces[(len(pieces) + 1) // 2 :])
+                else:
+                    quantise(0, BLOCKS[nxt][2])
+                    quantise(BLOCKS[nxt][2], ROWS * BLOCKS[nxt][2])
             for part in range(2):
                 if t == X1_QUANT[part]:
                     quantise_x(1, part)

@@ -47,7 +47,7 @@ def tile_localconvolution_kernel(tc, x, weight, grad_out, out):
 
         x_view = []
         for half in range(2):
-            x_t = raw.tile([P, PACK, C_HALF * H * W], BF16, name="xraw%d" % half)
+            x_t = raw.tile([P, PACK, C_HALF * H * W], BF16, name="xraw%d" % half, align_bytes=256)
             nc.sync.dma_start(
                 out=x_t[:],
                 in_=x[:, half * C_HALF : (half + 1) * C_HALF].rearrange(
@@ -57,7 +57,7 @@ def tile_localconvolution_kernel(tc, x, weight, grad_out, out):
             x_view.append(x_t[:].rearrange("p t (c h w) -> p h c t w", c=C_HALF, h=H, w=W))
         graw = []
         for lo, hi in ((0, P), (P, 2 * P), (2 * P, O)):
-            g_t = raw.tile([P, PACK, (hi - lo) * IJ], BF16, name="graw%d" % lo)
+            g_t = raw.tile([P, PACK, (hi - lo) * IJ], BF16, name="graw%d" % lo, align_bytes=256)
             nc.sync.dma_start(
                 out=g_t[:],
                 in_=grad_out[:, lo:hi].rearrange("(p t) o i j -> p t (o i j)", t=PACK),
@@ -136,7 +136,7 @@ def tile_localconvolution_kernel(tc, x, weight, grad_out, out):
             i = t % ROWS
             gc, gs = homes[t // ROWS]
             share = V_SHARE[t]
-            res_t = res.tile([P, r_n, C * KH * KW], F32, tag="res")
+            res_t = res.tile([P, r_n, C * KH * KW], F32, tag="res", align_bytes=256)
             for r in range(r_n):
                 m = i * r_n + r
                 for w in range(2):

@@ -28,7 +28,7 @@ C_HALF = C // 2
 FLOPS = 2 * ROWS * COLS * O * C * KH * KW * B
 BYTES = 2 * B * C * H * W + 2 * B * O * ROWS * COLS + 4 * ROWS * COLS * O * C * KH * KW
 
-V_SHARE = [0, 0, 0, 0, 0, 0, 0, 1, 0, 0, 0, 0, 0, 0, 0, 0, 1, 1, 1, 1, 2]
+V_SHARE = [0, 0, 0, 0, 0, 0, 1, 1, 1, 0, 0, 0, 0, 0, 0, 2, 2, 2, 2, 2, 2]
 X1_QUANT = (1, 2)
 X2_ROWS = (9, 10, 11, 12, 13, 13)
 X2_QUANT = (13, 14)

@@ -32,6 +32,7 @@ V_SHARE = [0, 0, 0, 0, 0, 0, 1, 1, 1, 0, 0, 0, 0, 0, 0, 2, 2, 2, 2, 2, 2]
 X1_QUANT = (1, 2)
 X2_ROWS = (9, 10, 11, 12, 13, 13)
 X2_QUANT = (13, 14)
+JOINED = (15, 18)
 BLOCKS = ((0, 0, 1), (0, P, 1), (1, 0, 2), (0, 2 * P, 2), (1, 2 * P, 2), (2, 0, 2), (2, 2 * P, 2))
 
 
@@ -42,7 +43,8 @@ def tile_localconvolution_kernel(tc, x, weight, grad_out, out):
         raw = ctx.enter_context(tc.tile_pool(name="raw", bufs=1))
         keep = ctx.enter_context(tc.tile_pool(name="keep", bufs=1))
         gstage = ctx.enter_context(tc.tile_pool(name="gstage", bufs=2))
-        res = ctx.enter_context(tc.tile_pool(name="res", bufs=8))
+        res = ctx.enter_context(tc.tile_pool(name="res", bufs=5))
+        res2 = ctx.enter_context(tc.tile_pool(name="res2", bufs=2))
         psum = ctx.enter_context(tc.psum_pool(name="psum", bufs=8))
 
         x_view = []
@@ -131,12 +133,22 @@ def tile_localconvolution_kernel(tc, x, weight, grad_out, out):
             for dst_ap, src_ap in pieces:
                 nc.vector.tensor_copy(out=dst_ap, in_=src_ap)
 
+        joined = []
+
         def unit(t):
             j, o0, r_n = BLOCKS[t // ROWS]
             i = t % ROWS
             gc, gs = homes[t // ROWS]
             share = V_SHARE[t]
-            res_t = res.tile([P, r_n, C * KH * KW], F32, tag="res", align_bytes=256)
+            if t in JOINED:
+                pair_t = res2.tile([P, 2, r_n, C * KH * KW], F32, tag="res2", align_bytes=256)
+                joined.append(pair_t)
+                res_ap = pair_t[:, 0]
+            elif t - 1 in JOINED:
+                res_ap = joined[-1][:, 1]
+            else:
+                res_t = res.tile([P, r_n, C * KH * KW], F32, tag="res", align_bytes=256)
+                res_ap = res_t[:]
             for r in range(r_n):
                 m = i * r_n + r
                 for w in range(2):
@@ -154,14 +166,24 @@ def tile_localconvolution_kernel(tc, x, weight, grad_out, out):
                     on_vector = 2 * r + w >= 2 * r_n - share
                     copy = nc.vector.tensor_copy if on_vector else nc.scalar.copy
                     copy(
-                        out=res_t[:, r].rearrange("p (c u v) -> p c u v", c=C, u=KH, v=KW)[
+                        out=res_ap[:, r].rearrange("p (c u v) -> p c u v", c=C, u=KH, v=KW)[
                             :, :, 2 * w : 2 * w + 2, :
                         ],
                         in_=acc[:].rearrange("p (u c v) -> p c u v", u=2, c=C, v=KW),
                     )
+            if t in JOINED:
+                return
+            if t - 1 in JOINED:
+                nc.sync.dma_start(
+                    out=out[i - 1 : i + 1, j, o0 : o0 + r_n * P].rearrange(
+                        "i (q r) c u v -> q i (r c u v)", r=r_n
+                    ),
+                    in_=joined[-1][:].rearrange("p i r n -> p i (r n)"),
+                )
+                return
             nc.sync.dma_start(
                 out=out[i, j, o0 : o0 + r_n * P].rearrange("(q r) c u v -> q r (c u v)", r=r_n),
-                in_=res_t[:],
+                in_=res_ap,
             )
 
         for half in range(2):

from contextlib import ExitStack

import concourse.mybir as mybir

F32 = mybir.dt.float32
BF16 = mybir.dt.bfloat16
U32 = mybir.dt.uint32
U8 = mybir.dt.uint8
E4M3X4 = mybir.dt.float8_e4m3fn_x4
E5M2X4 = mybir.dt.float8_e5m2_x4

P = 128
PACK = 4
B = 512
C = 64
O = 512
ROWS = 3
COLS = 3
KH = 4
KW = 4
H = 6
W = 6
N_WIN = 512
ROW_COLS = C * KW
IJ = ROWS * COLS
C_HALF = C // 2

FLOPS = 2 * ROWS * COLS * O * C * KH * KW * B
BYTES = 2 * B * C * H * W + 2 * B * O * ROWS * COLS + 4 * ROWS * COLS * O * C * KH * KW

V_SHARE = [0, 0, 0, 0, 0, 0, 1, 1, 1, 0, 0, 0, 0, 0, 0, 2, 2, 2, 2, 2, 2]
X1_QUANT = (1, 2)
X2_ROWS = (9, 10, 11, 12, 13, 13)
X2_QUANT = (13, 14)
JOINED = (15, 18)
BLOCKS = ((0, 0, 1), (0, P, 1), (1, 0, 2), (0, 2 * P, 2), (1, 2 * P, 2), (2, 0, 2), (2, 2 * P, 2))


def tile_localconvolution_kernel(tc, x, weight, grad_out, out):
    nc = tc.nc
    with ExitStack() as ctx:
        ctx.enter_context(tc.manual_schedule())
        raw = ctx.enter_context(tc.tile_pool(name="raw", bufs=1))
        keep = ctx.enter_context(tc.tile_pool(name="keep", bufs=1))
        gstage = ctx.enter_context(tc.tile_pool(name="gstage", bufs=2))
        res = ctx.enter_context(tc.tile_pool(name="res", bufs=5))
        res2 = ctx.enter_context(tc.tile_pool(name="res2", bufs=2))
        psum = ctx.enter_context(tc.psum_pool(name="psum", bufs=8))

        x_view = []
        for half in range(2):
            x_t = raw.tile([P, PACK, C_HALF * H * W], BF16, name="xraw%d" % half, align_bytes=256)
            nc.sync.dma_start(
                out=x_t[:],
                in_=x[:, half * C_HALF : (half + 1) * C_HALF].rearrange(
                    "(p t) c h w -> p t (c h w)", t=PACK
                ),
            )
            x_view.append(x_t[:].rearrange("p t (c h w) -> p h c t w", c=C_HALF, h=H, w=W))
        graw = []
        for lo, hi in ((0, P), (P, 2 * P), (2 * P, O)):
            g_t = raw.tile([P, PACK, (hi - lo) * IJ], BF16, name="graw%d" % lo, align_bytes=256)
            nc.sync.dma_start(
                out=g_t[:],
                in_=grad_out[:, lo:hi].rearrange("(p t) o i j -> p t (o i j)", t=PACK),
            )
            graw.append(g_t)

        xg = []
        xcodes = []
        xscales = []
        for j in range(COLS):
            xg.append(
                (
                    keep.tile([P, 4, C, KW, PACK], BF16, name="xga%d" % j, align_bytes=64),
                    keep.tile([P, 2, C, KW, PACK], BF16, name="xgb%d" % j, align_bytes=64),
                )
            )
            xcodes.append(keep.tile([P, H * ROW_COLS], U32, name="xcodes%d" % j, align_bytes=64))
            xscales.append(keep.tile([P, H * ROW_COLS], U8, name="xscales%d" % j, align_bytes=64))

        def regroup_x(copy, j, h, half):
            part = xg[j][h // 4]
            copy(
                out=part[:, h % 4, half * C_HALF : (half + 1) * C_HALF].rearrange(
                    "p c v t -> p c t v"
                ),
                in_=x_view[half][:, h, :, :, j : j + KW],
            )

        def quantise_x(j, part):
            lo = 0 if part == 0 else 4 * ROW_COLS
            hi = 4 * ROW_COLS if part == 0 else H * ROW_COLS
            nc.vector.quantize_mx(
                out=xcodes[j][:, lo:hi].bitcast(E4M3X4),
                scales=xscales[j][:, lo:hi],
                in_=xg[j][part][:].rearrange("p r c v t -> p (r c v t)"),
            )

        homes = []

        def prep_ops(b):
            j, o0, r_n = BLOCKS[b]
            gg = gstage.tile([P, ROWS * r_n, P, PACK], BF16, name="gg%d" % b, tag="gg%d" % r_n, align_bytes=64)
            gc = keep.tile([P, ROWS * r_n * P], U32, name="gc%d" % b, align_bytes=64)
            gs = keep.tile([P, ROWS * r_n * P], U8, name="gs%d" % b, align_bytes=64)
            homes.append((gc, gs))
            dst = gg[:].rearrange("p (i r) q t -> p r q t i", i=ROWS, r=r_n)
            pieces = []
            if o0 == 2 * P:
                sources = ((graw[2], 0, P),)
            elif r_n == 1:
                sources = ((graw[o0 // P], 0, P),)
            else:
                sources = ((graw[0], 0, P // 2), (graw[1], P // 2, P))
            for g_t, q_lo, q_hi in sources:
                src = g_t[:].rearrange(
                    "p t (q r i j) -> p r j q t i", q=q_hi - q_lo, r=r_n, i=ROWS, j=COLS
                )
                for r in range(r_n):
                    pieces.append((dst[:, r, q_lo:q_hi], src[:, r, j]))

            def quantise(lo, hi):
                nc.vector.quantize_mx(
                    out=gc[:, lo * P : hi * P].bitcast(E5M2X4),
                    scales=gs[:, lo * P : hi * P],
                    in_=gg[:, lo:hi].rearrange("p n q t -> p (n q t)"),
                )

            return pieces, quantise

        def regroup_g(pieces):
            for dst_ap, src_ap in pieces:
                nc.vector.tensor_copy(out=dst_ap, in_=src_ap)

        joined = []

        def unit(t):
            j, o0, r_n = BLOCKS[t // ROWS]
            i = t % ROWS
            gc, gs = homes[t // ROWS]
            share = V_SHARE[t]
            if t in JOINED:
                pair_t = res2.tile([P, 2, r_n, C * KH * KW], F32, tag="res2", align_bytes=256)
                joined.append(pair_t)
                res_ap = pair_t[:, 0]
            elif t - 1 in JOINED:
                res_ap = joined[-1][:, 1]
            else:
                res_t = res.tile([P, r_n, C * KH * KW], F32, tag="res", align_bytes=256)
                res_ap = res_t[:]
            for r in range(r_n):
                m = i * r_n + r
                for w in range(2):
                    acc = psum.tile([P, N_WIN], F32, tag="acc")
                    lo = (i + 2 * w) * ROW_COLS
                    nc.tensor.matmul_mx(
                        out=acc[:],
                        lhsT=gc[:, m * P : (m + 1) * P].bitcast(E5M2X4),
                        lhsT_scale=gs[:, m * P : (m + 1) * P],
                        rhs=xcodes[j][:, lo : lo + N_WIN].bitcast(E4M3X4),
                        rhs_scale=xscales[j][:, lo : lo + N_WIN],
                        start=True,
                        stop=True,
                    )
                    on_vector = 2 * r + w >= 2 * r_n - share
                    copy = nc.vector.tensor_copy if on_vector else nc.scalar.copy
                    copy(
                        out=res_ap[:, r].rearrange("p (c u v) -> p c u v", c=C, u=KH, v=KW)[
                            :, :, 2 * w : 2 * w + 2, :
                        ],
                        in_=acc[:].rearrange("p (u c v) -> p c u v", u=2, c=C, v=KW),
                    )
            if t in JOINED:
                return
            if t - 1 in JOINED:
                nc.sync.dma_start(
                    out=out[i - 1 : i + 1, j, o0 : o0 + r_n * P].rearrange(
                        "i (q r) c u v -> q i (r c u v)", r=r_n
                    ),
                    in_=joined[-1][:].rearrange("p i r n -> p i (r n)"),
                )
                return
            nc.sync.dma_start(
                out=out[i, j, o0 : o0 + r_n * P].rearrange("(q r) c u v -> q r (c u v)", r=r_n),
                in_=res_ap,
            )

        for half in range(2):
            for h in range(H):
                regroup_x(nc.vector.tensor_copy, 0, h, half)
        for half in range(2):
            for h in range(H):
                regroup_x(nc.scalar.copy, 1, h, half)
        quantise_x(0, 0)
        quantise_x(0, 1)
        pieces, quantise = prep_ops(0)
        regroup_g(pieces)
        quantise(0, BLOCKS[0][2])
        quantise(BLOCKS[0][2], ROWS * BLOCKS[0][2])
        x2_row = 0
        for t in range(ROWS * len(BLOCKS)):
            nxt = t // ROWS + 1
            pos = t % ROWS
            if nxt < len(BLOCKS):
                if pos == 0:
                    pieces, quantise = prep_ops(nxt)
                    regroup_g(pieces[: (len(pieces) + 1) // 2])
                elif pos == 1:
                    regroup_g(pieces[(len(pieces) + 1) // 2 :])
                else:
                    quantise(0, BLOCKS[nxt][2])
                    quantise(BLOCKS[nxt][2], ROWS * BLOCKS[nxt][2])
            for part in range(2):
                if t == X1_QUANT[part]:
                    quantise_x(1, part)
            for step in X2_ROWS:
                if step == t:
                    regroup_x(nc.vector.tensor_copy, 2, x2_row, 0)
                    regroup_x(nc.vector.tensor_copy, 2, x2_row, 1)
                    x2_row += 1
            for part in range(2):
                if t == X2_QUANT[part]:
                    quantise_x(2, part)
            unit(t)
